import numpy as np
import ml_dtypes


def mxq(x, axis, fmt="e4m3"):
    dtype, down = {"e4m3": (ml_dtypes.float8_e4m3fn, 7), "e5m2": (ml_dtypes.float8_e5m2, 14)}[fmt]
    v = np.moveaxis(np.asarray(x, np.float32).astype(ml_dtypes.bfloat16).astype(np.float64), axis, -1)
    blocks = v.reshape(v.shape[:-1] + (-1, 32))
    amax = np.abs(blocks).max(-1, keepdims=True)
    byte = np.maximum(np.where(amax > 0, np.frexp(amax)[1] - 1 + 127, 0) - down, 1)
    scale = np.exp2(byte - 127.0)
    codes = (blocks / scale).astype(np.float32).astype(dtype).astype(np.float64)
    return np.moveaxis((codes * scale).reshape(v.shape), -1, axis)


WIDE = False


def mx_kscale(k):
    if not WIDE:
        return np.ones(k)
    levels = np.array([10, -10, 5, -5, 0])
    if k % 512:
        return np.exp2(np.random.permutation(np.resize(levels, k // 32))).repeat(32)
    a = np.empty((k // 512, 16))
    for p in range(k // 512):
        a[p, :8] = np.random.permutation(np.resize(levels, 8))
        for g in range(8):
            far = levels[np.abs(levels - a[p, g]) >= 10]
            a[p, g + 8] = far[np.random.randint(len(far))]
    return np.exp2(a.ravel()).repeat(32)


BF16 = ml_dtypes.bfloat16


def bf(x):
    return np.asarray(x, np.float32).astype(BF16)


def f64(x):
    return np.asarray(x).astype(np.float64)


B, S, D, H, C = 1, 1024, 1024, 1024, 512


def setup_inputs():
    s, t = mx_kscale(H), mx_kscale(S)
    return {"q": bf(np.random.standard_normal((B, S, H)) * 0.6 * s),
            "k": bf(np.random.standard_normal((B, S, H)) * 0.6 / s * t[:, None]),
            "v": bf(np.random.standard_normal((B, S, H)) * 0.6 / t[:, None]),
            "decay": bf(np.random.uniform(0.5, 1.5, S) * 2.0 / S)}


def reference(q, k, v, decay):
    qq = mxq(f64(q), 2, "e4m3")
    kq = mxq(f64(k), 2, "e4m3")
    vq = mxq(f64(v), 1, "e4m3")
    idx = np.arange(S)
    diff = f64(np.abs(idx[None, :] - idx[:, None]))
    dm = np.exp(-f64(decay)[None, :] * diff) * np.tril(np.ones((S, S)))
    out = np.zeros((B, S, H))
    for r in range(0, S, C):
        e = r + C
        sc = (qq[:, r:e] @ kq[:, :e].transpose(0, 2, 1)) * dm[r:e, :e]
        sc = sc / np.sqrt(H)
        out[:, r:e] = mxq(sc, 2, "e4m3") @ vq[:, :e]
    return out

@@ -1,0 +1,270 @@
+from contextlib import ExitStack
+
+import concourse.mybir as mybir
+from concourse.masks import make_identity
+
+F32 = mybir.dt.float32
+BF16 = mybir.dt.bfloat16
+I32 = mybir.dt.int32
+U32 = mybir.dt.uint32
+U8 = mybir.dt.uint8
+FP8X4 = mybir.dt.float8_e4m3fn_x4
+ALU = mybir.AluOpType
+ACT = mybir.ActivationFunctionType
+
+P = 128
+S = 1024
+H = 1024
+CHUNK = 512
+TILES = CHUNK // P
+BANK = 512
+FAR = 1e30
+FLOPS = 2 * 2 * H * (CHUNK * CHUNK + CHUNK * 2 * CHUNK)
+
+
+def tile_simplifiedretnet_pa_kernel(tc, q, k, v, decay, out):
+    nc = tc.nc
+    dram = {
+        "q": q.rearrange("b s h -> (b s) h"),
+        "k": k.rearrange("b s h -> (b s) h"),
+        "v": v.rearrange("b s h -> (b s) h"),
+    }
+    out2 = out.rearrange("b s h -> (b s) h")
+
+    with ExitStack() as stack:
+        keep = stack.enter_context(tc.tile_pool(name="keep", bufs=1))
+        psum = stack.enter_context(tc.psum_pool(name="psum", bufs=8))
+        stack.enter_context(tc.manual_schedule())
+
+        raw = {}
+        grouped = {}
+        banks = {}
+        codes = {}
+        planes = {}
+        tables = {}
+        stages = {}
+
+        def load_rows(kind, n):
+            raw[(kind, n)] = keep.tile([P, H], BF16, name="raw_%s%d" % (kind, n))
+            if kind == "q":
+                rows = dram["q"][P * n : P * (n + 1), :]
+            else:
+                c = n // TILES
+                rows = dram["k"][CHUNK * c : CHUNK * (c + 1), :].rearrange("(p t) h -> t p h", t=TILES)[n % TILES]
+            nc.sync.dma_start(out=raw[(kind, n)][:], in_=rows)
+
+        def load_values(g):
+            raw[("v", g)] = keep.tile([P, TILES * H], BF16, name="raw_v%d" % g)
+            view = raw[("v", g)][:].rearrange("p (t h) -> p t h", t=TILES)
+            rows = dram["v"][CHUNK * g : CHUNK * (g + 1), :].rearrange("(p t) h -> p t h", t=TILES)
+            for half in range(2):
+                nc.sync.dma_start(out=view[:, 2 * half : 2 * half + 2, :], in_=rows[:, 2 * half : 2 * half + 2, :])
+
+        def table(c, g, t):
+            if (c, g) not in tables:
+                tables[(c, g)] = keep.tile([P, TILES * CHUNK], F32, name="m%d%d" % (c, g))
+            y0 = (0 if g == c else CHUNK) + TILES - 1 - t
+            nc.scalar.activation(
+                out=tables[(c, g)][:, CHUNK * t : CHUNK * (t + 1)], in_=dist[:, y0 : y0 + CHUNK], func=ACT.Exp,
+                scale=negd[:, TILES * g + t : TILES * g + t + 1],
+            )
+
+        def flip(kind, n, engine):
+            words = raw[(kind, n)][:].bitcast(F32)
+            bank = psum.tile([P, BANK], F32, name="bank")
+            for w in range(4):
+                nc.tensor.transpose(bank[:, P * w : P * (w + 1)], words[:, 2 * P * (w // 2) + w % 2 : 2 * P * (w // 2 + 1) : 2], ident[:])
+            grouped[(kind, n)] = keep.tile([P, H], BF16, name="g_%s%d" % (kind, n), align_bytes=64)
+            dst = grouped[(kind, n)][:].bitcast(F32).rearrange("p (g r u) -> p g r u", g=2, u=2)
+            src = bank[:].rearrange("p (g u r) -> p g r u", g=2, u=2)
+            if engine == "vector":
+                nc.vector.tensor_copy(out=dst, in_=src)
+            else:
+                nc.scalar.copy(out=dst, in_=src)
+            if n < 6:
+                keep_busy(1, BANK // 2)
+
+        def quantise(kind, n):
+            width = grouped[(kind, n)].shape[1]
+            cd = keep.tile([P, width // 4], U32, name="c_%s%d" % (kind, n), align_bytes=64)
+            pl = keep.tile([P, width // 4], U8, name="p_%s%d" % (kind, n), align_bytes=64)
+            nc.vector.quantize_mx(out=cd[:].bitcast(FP8X4), scales=pl[:], in_=grouped[(kind, n)][:])
+            codes[(kind, n)] = cd
+            planes[(kind, n)] = pl
+
+        def regroup_values(g, hh):
+            grouped[("v", 2 * g + hh)] = keep.tile([P, 4 * BANK], BF16, name="g_v%d%d" % (g, hh), align_bytes=64)
+            src = raw[("v", g)][:].rearrange("p (t h) -> p t h", t=TILES)[:, :, BANK * hh : BANK * (hh + 1)]
+            nc.vector.tensor_copy(
+                out=grouped[("v", 2 * g + hh)][:].rearrange("p (c i t) -> p c t i", i=4, t=4),
+                in_=src.rearrange("p t (c i) -> p c t i", i=4),
+            )
+
+        def mx(dst, left, lcols, right, rcols, start, stop):
+            nc.tensor.matmul_mx(
+                out=dst,
+                lhsT=codes[left][:, lcols].bitcast(FP8X4), lhsT_scale=planes[left][:, lcols],
+                rhs=codes[right][:, rcols].bitcast(FP8X4), rhs_scale=planes[right][:, rcols],
+                start=start, stop=stop,
+            )
+
+        def scores(c, g, a):
+            bank = psum.tile([P, BANK], F32, name="bank")
+            for t in range(TILES):
+                for hp in range(2):
+                    cols = slice(P * hp, P * (hp + 1))
+                    mx(bank[:, P * t : P * (t + 1)], ("k", TILES * g + t), cols, ("q", TILES * c + a), cols, hp == 0, hp == 1)
+            m = tables[(c, g)][:].rearrange("p (t i) -> p t i", t=TILES)
+            part = grouped[("s", TILES * c + a)][:, CHUNK * g : CHUNK * (g + 1)]
+            nc.vector.scalar_tensor_tensor(
+                out=part.rearrange("p (i t) -> p i t", t=TILES),
+                in0=bank[:].rearrange("p (t i) -> p i t", t=TILES),
+                scalar=1.0 / 32.0,
+                in1=m[:, :, P * a : P * (a + 1)].rearrange("p t i -> p i t"),
+                op0=ALU.mult, op1=ALU.mult,
+            )
+
+        def outputs(c, a, hh, engine):
+            acc = psum.tile([P, BANK], F32, name="bank")
+            for g in range(c + 1):
+                mx(acc[:], ("s", TILES * c + a), slice(P * g, P * (g + 1)), ("v", 2 * g + hh), slice(0, BANK), g == 0, g == c)
+            stages[(c, a, hh)] = keep.tile([P, BANK], F32, name="o%d%d%d" % (c, a, hh))
+            if engine == "vector":
+                nc.vector.tensor_copy(out=stages[(c, a, hh)][:], in_=acc[:])
+            else:
+                nc.scalar.copy(out=stages[(c, a, hh)][:], in_=acc[:])
+            row = CHUNK * c + P * a
+            nc.sync.dma_start(out=out2[row : row + P, BANK * hh : BANK * (hh + 1)], in_=stages[(c, a, hh)][:])
+
+        def keep_busy(count, width):
+            bank = psum.tile([P, BANK], F32, name="bank")
+            for i in range(count):
+                nc.tensor.matmul(out=bank[:, 0:width], lhsT=spin[:, 0:P], rhs=spin[:, 0:width], start=True, stop=True)
+
+        spin = keep.tile([P, BANK], BF16, name="spin")
+        nc.vector.memset(spin[:].bitcast(I32), 0)
+        keep_busy(6, BANK)
+        dec = keep.tile([P, 2 * TILES], BF16, name="dec")
+        with nc.allow_non_contiguous_dma(reason="1024 decay rates, one key to a partition"):
+            nc.scalar.dma_start(out=dec[:].rearrange("p (g t) -> p g t", g=2), in_=decay.rearrange("(g p t) -> p g t", g=2, t=TILES))
+        for n in range(TILES):
+            load_rows("k", n)
+        for n in range(TILES):
+            load_rows("q", n)
+        load_values(0)
+        for n in range(TILES, 2 * TILES):
+            load_rows("q", n)
+        for n in range(TILES, 2 * TILES):
+            load_rows("k", n)
+        load_values(1)
+
+        warm = keep.tile([P, 1], F32, name="warm")
+        nc.vector.memset(warm[:], 0.0)
+        warm2 = keep.tile([P, 1], F32, name="warm2")
+        nc.scalar.activation(out=warm2[:], in_=warm[:], func=ACT.Exp)
+        ident = keep.tile([P, P], F32, name="ident")
+        make_identity(nc, ident[:])
+        for c in range(2):
+            for a in range(TILES):
+                n = TILES * c + a
+                grouped[("s", n)] = keep.tile([P, (c + 1) * CHUNK], BF16, name="g_s%d" % n, align_bytes=64)
+        dist = keep.tile([P, S + TILES - 1], F32, name="dist")
+        nc.gpsimd.iota(dist[:], pattern=[[1, S + TILES - 1]], base=1 - TILES, channel_multiplier=-TILES,
+            allow_small_or_imprecise_dtypes=True,
+        )
+        nc.gpsimd.affine_select(
+            out=dist[:, 0:CHUNK], in_=dist[:, 0:CHUNK], pattern=[[1, CHUNK]], compare_op=ALU.is_ge, fill=FAR,
+            base=1 - TILES, channel_multiplier=-TILES,
+        )
+        negd = keep.tile([P, 2 * TILES], F32, name="negd")
+        nc.vector.tensor_scalar_mul(out=negd[:], in0=dec[:], scalar1=-1.0)
+
+        flip("k", 0, "vector")
+        table(0, 0, 0)
+        table(0, 0, 1)
+        flip("k", 1, "scalar")
+        flip("k", 2, "vector")
+        quantise("k", 0)
+        table(0, 0, 2)
+        flip("k", 3, "scalar")
+        quantise("k", 1)
+        flip("q", 0, "vector")
+        quantise("k", 2)
+        quantise("k", 3)
+        quantise("q", 0)
+        table(0, 0, 3)
+        flip("q", 1, "scalar")
+        scores(0, 0, 0)
+        flip("q", 2, "scalar")
+        quantise("q", 1)
+        scores(0, 0, 1)
+        flip("q", 3, "scalar")
+        quantise("q", 2)
+        quantise("s", 0)
+        scores(0, 0, 2)
+        quantise("s", 1)
+        quantise("q", 3)
+        scores(0, 0, 3)
+        table(1, 0, 0)
+        table(1, 0, 1)
+        regroup_values(0, 0)
+        quantise("s", 2)
+        regroup_values(0, 1)
+        for n in (4, 5):
+            flip("q", n, "scalar")
+        quantise("v", 0)
+        quantise("s", 3)
+        quantise("v", 1)
+        table(1, 0, 2)
+        table(1, 0, 3)
+        quantise("q", 4)
+        quantise("q", 5)
+
+        outputs(0, 0, 0, "scalar")
+        outputs(0, 0, 1, "scalar")
+        scores(1, 0, 0)
+        flip("q", 6, "scalar")
+        flip("q", 7, "scalar")
+        outputs(0, 1, 0, "scalar")
+        outputs(0, 1, 1, "scalar")
+        scores(1, 0, 1)
+        quantise("q", 6)
+        quantise("q", 7)
+        for n in (4, 5):
+            flip("k", n, "scalar")
+        table(1, 1, 0)
+        outputs(0, 2, 0, "scalar")
+        scores(1, 0, 2)
+        quantise("k", 4)
+        quantise("k", 5)
+        for n in (6, 7):
+            flip("k", n, "scalar")
+        table(1, 1, 1)
+        outputs(0, 2, 1, "scalar")
+        scores(1, 0, 3)
+        quantise("k", 6)
+        quantise("k", 7)
+        table(1, 1, 2)
+        table(1, 1, 3)
+        regroup_values(1, 0)
+        scores(1, 1, 0)
+        outputs(0, 3, 0, "scalar")
+        outputs(0, 3, 1, "scalar")
+        regroup_values(1, 1)
+        scores(1, 1, 1)
+        quantise("v", 2)
+        quantise("s", 4)
+        quantise("v", 3)
+        scores(1, 1, 2)
+        outputs(1, 0, 0, "scalar")
+        outputs(1, 0, 1, "scalar")
+        quantise("s", 5)
+        scores(1, 1, 3)
+        quantise("s", 6)
+        outputs(1, 1, 0, "scalar")
+        outputs(1, 1, 1, "scalar")
+        quantise("s", 7)
+        outputs(1, 2, 0, "scalar")
+        outputs(1, 2, 1, "vector")
+        outputs(1, 3, 0, "vector")
+        outputs(1, 3, 1, "scalar")

@@ -37,8 +37,8 @@ def tile_simplifiedretnet_pa_kernel(tc, q, k, v, decay, out):
         stack.enter_context(tc.manual_schedule())
 
         raw = {}
-        grouped = {}
         banks = {}
+        grouped = {}
         codes = {}
         planes = {}
         tables = {}
@@ -53,12 +53,13 @@ def tile_simplifiedretnet_pa_kernel(tc, q, k, v, decay, out):
                 rows = dram["k"][CHUNK * c : CHUNK * (c + 1), :].rearrange("(p t) h -> t p h", t=TILES)[n % TILES]
             nc.sync.dma_start(out=raw[(kind, n)][:], in_=rows)
 
-        def load_values(g):
-            raw[("v", g)] = keep.tile([P, TILES * H], BF16, name="raw_v%d" % g)
-            view = raw[("v", g)][:].rearrange("p (t h) -> p t h", t=TILES)
+        def load_values(g, hh):
+            raw[("v", 2 * g + hh)] = keep.tile([P, TILES * BANK], BF16, name="raw_v%d%d" % (g, hh))
             rows = dram["v"][CHUNK * g : CHUNK * (g + 1), :].rearrange("(p t) h -> p t h", t=TILES)
-            for half in range(2):
-                nc.sync.dma_start(out=view[:, 2 * half : 2 * half + 2, :], in_=rows[:, 2 * half : 2 * half + 2, :])
+            nc.sync.dma_start(
+                out=raw[("v", 2 * g + hh)][:].rearrange("p (t h) -> p t h", t=TILES),
+                in_=rows[:, :, BANK * hh : BANK * (hh + 1)],
+            )
 
         def table(c, g, t):
             if (c, g) not in tables:
@@ -69,20 +70,23 @@ def tile_simplifiedretnet_pa_kernel(tc, q, k, v, decay, out):
                 scale=negd[:, TILES * g + t : TILES * g + t + 1],
             )
 
-        def flip(kind, n, engine):
+        def turn(kind, n):
             words = raw[(kind, n)][:].bitcast(F32)
             bank = psum.tile([P, BANK], F32, name="bank")
             for w in range(4):
-                nc.tensor.transpose(bank[:, P * w : P * (w + 1)], words[:, 2 * P * (w // 2) + w % 2 : 2 * P * (w // 2 + 1) : 2], ident[:])
+                nc.tensor.transpose(
+                    bank[:, P * w : P * (w + 1)], words[:, 2 * P * (w // 2) + w % 2 : 2 * P * (w // 2 + 1) : 2], ident[:]
+                )
+            banks[(kind, n)] = bank
+
+        def fetch(kind, n, engine):
             grouped[(kind, n)] = keep.tile([P, H], BF16, name="g_%s%d" % (kind, n), align_bytes=64)
             dst = grouped[(kind, n)][:].bitcast(F32).rearrange("p (g r u) -> p g r u", g=2, u=2)
-            src = bank[:].rearrange("p (g u r) -> p g r u", g=2, u=2)
+            src = banks[(kind, n)][:].rearrange("p (g u r) -> p g r u", g=2, u=2)
             if engine == "vector":
                 nc.vector.tensor_copy(out=dst, in_=src)
             else:
                 nc.scalar.copy(out=dst, in_=src)
-            if n < 6:
-                keep_busy(1, BANK // 2)
 
         def quantise(kind, n):
             width = grouped[(kind, n)].shape[1]
@@ -92,13 +96,14 @@ def tile_simplifiedretnet_pa_kernel(tc, q, k, v, decay, out):
             codes[(kind, n)] = cd
             planes[(kind, n)] = pl
 
-        def regroup_values(g, hh):
-            grouped[("v", 2 * g + hh)] = keep.tile([P, 4 * BANK], BF16, name="g_v%d%d" % (g, hh), align_bytes=64)
-            src = raw[("v", g)][:].rearrange("p (t h) -> p t h", t=TILES)[:, :, BANK * hh : BANK * (hh + 1)]
-            nc.vector.tensor_copy(
-                out=grouped[("v", 2 * g + hh)][:].rearrange("p (c i t) -> p c t i", i=4, t=4),
-                in_=src.rearrange("p t (c i) -> p c t i", i=4),
-            )
+        def regroup(n, engine="vector"):
+            grouped[("v", n)] = keep.tile([P, TILES * BANK], BF16, name="g_v%d" % n, align_bytes=64)
+            dst = grouped[("v", n)][:].rearrange("p (c i t) -> p c t i", i=4, t=4)
+            src = raw[("v", n)][:].rearrange("p (t c i) -> p c t i", t=4, i=4)
+            if engine == "vector":
+                nc.vector.tensor_copy(out=dst, in_=src)
+            else:
+                nc.scalar.copy(out=dst, in_=src)
 
         def mx(dst, left, lcols, right, rcols, start, stop):
             nc.tensor.matmul_mx(
@@ -114,25 +119,34 @@ def tile_simplifiedretnet_pa_kernel(tc, q, k, v, decay, out):
                 for hp in range(2):
                     cols = slice(P * hp, P * (hp + 1))
                     mx(bank[:, P * t : P * (t + 1)], ("k", TILES * g + t), cols, ("q", TILES * c + a), cols, hp == 0, hp == 1)
-            m = tables[(c, g)][:].rearrange("p (t i) -> p t i", t=TILES)
-            part = grouped[("s", TILES * c + a)][:, CHUNK * g : CHUNK * (g + 1)]
+            banks[(c, g, a)] = bank
+
+        def weigh(c, g, a):
+            n = TILES * c + a
+            if ("s", n) not in grouped:
+                grouped[("s", n)] = keep.tile([P, (c + 1) * CHUNK], BF16, name="g_s%d" % n, align_bytes=64)
+            part = grouped[("s", n)][:, CHUNK * g : CHUNK * (g + 1)]
+            m = tables[(c, g)][:].rearrange("p (t i) -> p i t", t=TILES)
             nc.vector.scalar_tensor_tensor(
                 out=part.rearrange("p (i t) -> p i t", t=TILES),
-                in0=bank[:].rearrange("p (t i) -> p i t", t=TILES),
+                in0=banks[(c, g, a)][:].rearrange("p (t i) -> p i t", t=TILES),
                 scalar=1.0 / 32.0,
-                in1=m[:, :, P * a : P * (a + 1)].rearrange("p t i -> p i t"),
+                in1=m[:, P * a : P * (a + 1), :],
                 op0=ALU.mult, op1=ALU.mult,
             )
 
-        def outputs(c, a, hh, engine):
+        def product(c, a, hh):
             acc = psum.tile([P, BANK], F32, name="bank")
             for g in range(c + 1):
                 mx(acc[:], ("s", TILES * c + a), slice(P * g, P * (g + 1)), ("v", 2 * g + hh), slice(0, BANK), g == 0, g == c)
+            banks[("o", c, a, hh)] = acc
+
+        def drain(c, a, hh, engine):
             stages[(c, a, hh)] = keep.tile([P, BANK], F32, name="o%d%d%d" % (c, a, hh))
             if engine == "vector":
-                nc.vector.tensor_copy(out=stages[(c, a, hh)][:], in_=acc[:])
+                nc.vector.tensor_copy(out=stages[(c, a, hh)][:], in_=banks[("o", c, a, hh)][:])
             else:
-                nc.scalar.copy(out=stages[(c, a, hh)][:], in_=acc[:])
+                nc.scalar.copy(out=stages[(c, a, hh)][:], in_=banks[("o", c, a, hh)][:])
             row = CHUNK * c + P * a
             nc.sync.dma_start(out=out2[row : row + P, BANK * hh : BANK * (hh + 1)], in_=stages[(c, a, hh)][:])
 
@@ -145,18 +159,30 @@ def tile_simplifiedretnet_pa_kernel(tc, q, k, v, decay, out):
         nc.vector.memset(spin[:].bitcast(I32), 0)
         keep_busy(6, BANK)
         dec = keep.tile([P, 2 * TILES], BF16, name="dec")
-        with nc.allow_non_contiguous_dma(reason="1024 decay rates, one key to a partition"):
-            nc.scalar.dma_start(out=dec[:].rearrange("p (g t) -> p g t", g=2), in_=decay.rearrange("(g p t) -> p g t", g=2, t=TILES))
-        for n in range(TILES):
-            load_rows("k", n)
-        for n in range(TILES):
-            load_rows("q", n)
-        load_values(0)
-        for n in range(TILES, 2 * TILES):
-            load_rows("q", n)
-        for n in range(TILES, 2 * TILES):
-            load_rows("k", n)
-        load_values(1)
+        with nc.allow_non_contiguous_dma(reason="1024 decay rates, four keys to a partition and chunk"):
+            nc.scalar.dma_start(
+                out=dec[:].rearrange("p (g t) -> p g t", g=2), in_=decay.rearrange("(g p t) -> p g t", g=2, t=TILES)
+            )
+        load_rows("k", 0)
+        load_rows("k", 1)
+        load_rows("k", 2)
+        load_rows("k", 3)
+        load_rows("q", 0)
+        load_rows("q", 1)
+        load_values(0, 0)
+        load_rows("q", 2)
+        load_rows("q", 3)
+        load_values(0, 1)
+        load_rows("q", 4)
+        load_rows("q", 5)
+        load_rows("q", 6)
+        load_rows("q", 7)
+        load_rows("k", 4)
+        load_rows("k", 5)
+        load_rows("k", 6)
+        load_rows("k", 7)
+        load_values(1, 0)
+        load_values(1, 1)
 
         warm = keep.tile([P, 1], F32, name="warm")
         nc.vector.memset(warm[:], 0.0)
@@ -164,107 +190,155 @@ def tile_simplifiedretnet_pa_kernel(tc, q, k, v, decay, out):
         nc.scalar.activation(out=warm2[:], in_=warm[:], func=ACT.Exp)
         ident = keep.tile([P, P], F32, name="ident")
         make_identity(nc, ident[:])
-        for c in range(2):
-            for a in range(TILES):
-                n = TILES * c + a
-                grouped[("s", n)] = keep.tile([P, (c + 1) * CHUNK], BF16, name="g_s%d" % n, align_bytes=64)
         dist = keep.tile([P, S + TILES - 1], F32, name="dist")
-        nc.gpsimd.iota(dist[:], pattern=[[1, S + TILES - 1]], base=1 - TILES, channel_multiplier=-TILES,
-            allow_small_or_imprecise_dtypes=True,
-        )
-        nc.gpsimd.affine_select(
-            out=dist[:, 0:CHUNK], in_=dist[:, 0:CHUNK], pattern=[[1, CHUNK]], compare_op=ALU.is_ge, fill=FAR,
-            base=1 - TILES, channel_multiplier=-TILES,
-        )
+        near = CHUNK + TILES - 1
+        for y0, y1 in ((0, near), (near, S + TILES - 1)):
+            nc.gpsimd.iota(
+                dist[:, y0:y1], pattern=[[1, y1 - y0]], base=y0 + 1 - TILES, channel_multiplier=-TILES,
+                allow_small_or_imprecise_dtypes=True,
+            )
+            if y0 == 0:
+                nc.gpsimd.affine_select(
+                    out=dist[:, y0:y1], in_=dist[:, y0:y1], pattern=[[1, y1 - y0]], compare_op=ALU.is_ge, fill=FAR,
+                    base=1 - TILES, channel_multiplier=-TILES,
+                )
         negd = keep.tile([P, 2 * TILES], F32, name="negd")
         nc.vector.tensor_scalar_mul(out=negd[:], in0=dec[:], scalar1=-1.0)
 
-        flip("k", 0, "vector")
+        turn("k", 0)
+        fetch("k", 0, "vector")
         table(0, 0, 0)
         table(0, 0, 1)
-        flip("k", 1, "scalar")
-        flip("k", 2, "vector")
-        quantise("k", 0)
+        keep_busy(1, 256)
+        turn("k", 1)
+        fetch("k", 1, "scalar")
         table(0, 0, 2)
-        flip("k", 3, "scalar")
+        keep_busy(1, 256)
+        turn("k", 2)
+        fetch("k", 2, "vector")
+        quantise("k", 0)
+        keep_busy(1, 256)
+        turn("k", 3)
+        fetch("k", 3, "scalar")
+        table(0, 0, 3)
         quantise("k", 1)
-        flip("q", 0, "vector")
+        keep_busy(1, 256)
+        turn("q", 0)
+        fetch("q", 0, "vector")
         quantise("k", 2)
+        keep_busy(1, 256)
+        turn("q", 1)
+        fetch("q", 1, "scalar")
         quantise("k", 3)
         quantise("q", 0)
-        table(0, 0, 3)
-        flip("q", 1, "scalar")
-        scores(0, 0, 0)
-        flip("q", 2, "scalar")
-        quantise("q", 1)
-        scores(0, 0, 1)
-        flip("q", 3, "scalar")
-        quantise("q", 2)
-        quantise("s", 0)
-        scores(0, 0, 2)
-        quantise("s", 1)
-        quantise("q", 3)
-        scores(0, 0, 3)
         table(1, 0, 0)
         table(1, 0, 1)
-        regroup_values(0, 0)
-        quantise("s", 2)
-        regroup_values(0, 1)
-        for n in (4, 5):
-            flip("q", n, "scalar")
-        quantise("v", 0)
-        quantise("s", 3)
-        quantise("v", 1)
         table(1, 0, 2)
+        scores(0, 0, 0)
+        turn("q", 2)
+        quantise("q", 1)
+        fetch("q", 2, "scalar")
         table(1, 0, 3)
+        regroup(0)
+        weigh(0, 0, 0)
+        scores(0, 0, 1)
+        turn("q", 3)
+        fetch("q", 3, "scalar")
+        quantise("v", 0)
+        quantise("q", 2)
+        table(1, 1, 0)
+        table(1, 1, 1)
+        weigh(0, 0, 1)
+        scores(0, 0, 2)
+        quantise("s", 0)
+        quantise("q", 3)
+        turn("q", 4)
+        turn("q", 5)
+        weigh(0, 0, 2)
+        fetch("q", 4, "scalar")
+        scores(0, 0, 3)
+        quantise("s", 1)
+        fetch("q", 5, "scalar")
+        regroup(1)
+        weigh(0, 0, 3)
         quantise("q", 4)
-        quantise("q", 5)
-
-        outputs(0, 0, 0, "scalar")
-        outputs(0, 0, 1, "scalar")
+        table(1, 1, 2)
+        turn("q", 6)
+        turn("q", 7)
         scores(1, 0, 0)
-        flip("q", 6, "scalar")
-        flip("q", 7, "scalar")
-        outputs(0, 1, 0, "scalar")
-        outputs(0, 1, 1, "scalar")
+        fetch("q", 6, "scalar")
+        fetch("q", 7, "scalar")
+        quantise("q", 5)
+        quantise("s", 2)
+        quantise("v", 1)
+        weigh(1, 0, 0)
         scores(1, 0, 1)
+        quantise("s", 3)
         quantise("q", 6)
         quantise("q", 7)
-        for n in (4, 5):
-            flip("k", n, "scalar")
-        table(1, 1, 0)
-        outputs(0, 2, 0, "scalar")
-        scores(1, 0, 2)
+        turn("k", 4)
+        turn("k", 5)
+        turn("k", 6)
+        turn("k", 7)
+        table(1, 1, 3)
+        fetch("k", 4, "scalar")
+        fetch("k", 5, "scalar")
+        weigh(1, 0, 1)
+        product(0, 0, 0)
+        product(0, 0, 1)
+        fetch("k", 6, "scalar")
+        fetch("k", 7, "scalar")
         quantise("k", 4)
         quantise("k", 5)
-        for n in (6, 7):
-            flip("k", n, "scalar")
-        table(1, 1, 1)
-        outputs(0, 2, 1, "scalar")
+        regroup(2)
+        scores(1, 0, 2)
         scores(1, 0, 3)
+        drain(0, 0, 0, "scalar")
+        drain(0, 0, 1, "scalar")
         quantise("k", 6)
         quantise("k", 7)
-        table(1, 1, 2)
-        table(1, 1, 3)
-        regroup_values(1, 0)
+        weigh(1, 0, 2)
+        product(0, 1, 0)
+        product(0, 1, 1)
+        drain(0, 1, 0, "scalar")
+        drain(0, 1, 1, "scalar")
+        regroup(3, "scalar")
         scores(1, 1, 0)
-        outputs(0, 3, 0, "scalar")
-        outputs(0, 3, 1, "scalar")
-        regroup_values(1, 1)
-        scores(1, 1, 1)
+        weigh(1, 0, 3)
         quantise("v", 2)
+        product(0, 2, 0)
+        scores(1, 1, 1)
+        product(0, 2, 1)
+        weigh(1, 1, 0)
+        drain(0, 2, 0, "scalar")
+        weigh(1, 1, 1)
         quantise("s", 4)
         quantise("v", 3)
         scores(1, 1, 2)
-        outputs(1, 0, 0, "scalar")
-        outputs(1, 0, 1, "scalar")
-        quantise("s", 5)
+        product(0, 3, 0)
+        drain(0, 2, 1, "scalar")
         scores(1, 1, 3)
+        product(0, 3, 1)
+        weigh(1, 1, 2)
+        product(1, 0, 0)
+        product(1, 0, 1)
+        quantise("s", 5)
+        drain(0, 3, 0, "scalar")
+        drain(0, 3, 1, "scalar")
+        weigh(1, 1, 3)
         quantise("s", 6)
-        outputs(1, 1, 0, "scalar")
-        outputs(1, 1, 1, "scalar")
+        product(1, 1, 0)
+        product(1, 1, 1)
         quantise("s", 7)
-        outputs(1, 2, 0, "scalar")
-        outputs(1, 2, 1, "vector")
-        outputs(1, 3, 0, "vector")
-        outputs(1, 3, 1, "scalar")
+        drain(1, 0, 0, "scalar")
+        drain(1, 0, 1, "vector")
+        product(1, 2, 0)
+        product(1, 2, 1)
+        drain(1, 1, 0, "scalar")
+        drain(1, 1, 1, "vector")
+        product(1, 3, 0)
+        product(1, 3, 1)
+        drain(1, 2, 0, "scalar")
+        drain(1, 2, 1, "vector")
+        drain(1, 3, 0, "scalar")
+        drain(1, 3, 1, "vector")

@@ -88,13 +88,14 @@ def tile_simplifiedretnet_pa_kernel(tc, q, k, v, decay, out):
             else:
                 nc.scalar.copy(out=dst, in_=src)
 
-        def quantise(kind, n):
-            width = grouped[(kind, n)].shape[1]
-            cd = keep.tile([P, width // 4], U32, name="c_%s%d" % (kind, n), align_bytes=64)
-            pl = keep.tile([P, width // 4], U8, name="p_%s%d" % (kind, n), align_bytes=64)
-            nc.vector.quantize_mx(out=cd[:].bitcast(FP8X4), scales=pl[:], in_=grouped[(kind, n)][:])
-            codes[(kind, n)] = cd
-            planes[(kind, n)] = pl
+        def quantise(*key):
+            width = grouped[key].shape[1]
+            name = "%s%d" % key if len(key) == 2 else "%s%d%d" % key
+            cd = keep.tile([P, width // 4], U32, name="c_" + name, align_bytes=64)
+            pl = keep.tile([P, width // 4], U8, name="p_" + name, align_bytes=64)
+            nc.vector.quantize_mx(out=cd[:].bitcast(FP8X4), scales=pl[:], in_=grouped[key][:])
+            codes[key] = cd
+            planes[key] = pl
 
         def regroup(n, engine="vector"):
             grouped[("v", n)] = keep.tile([P, TILES * BANK], BF16, name="g_v%d" % n, align_bytes=64)
@@ -123,9 +124,8 @@ def tile_simplifiedretnet_pa_kernel(tc, q, k, v, decay, out):
 
         def weigh(c, g, a):
             n = TILES * c + a
-            if ("s", n) not in grouped:
-                grouped[("s", n)] = keep.tile([P, (c + 1) * CHUNK], BF16, name="g_s%d" % n, align_bytes=64)
-            part = grouped[("s", n)][:, CHUNK * g : CHUNK * (g + 1)]
+            grouped[("s", n, g)] = keep.tile([P, CHUNK], BF16, name="g_s%d%d" % (n, g), align_bytes=64)
+            part = grouped[("s", n, g)][:]
             m = tables[(c, g)][:].rearrange("p (t i) -> p i t", t=TILES)
             nc.vector.scalar_tensor_tensor(
                 out=part.rearrange("p (i t) -> p i t", t=TILES),
@@ -135,11 +135,13 @@ def tile_simplifiedretnet_pa_kernel(tc, q, k, v, decay, out):
                 op0=ALU.mult, op1=ALU.mult,
             )
 
-        def product(c, a, hh):
-            acc = psum.tile([P, BANK], F32, name="bank")
-            for g in range(c + 1):
-                mx(acc[:], ("s", TILES * c + a), slice(P * g, P * (g + 1)), ("v", 2 * g + hh), slice(0, BANK), g == 0, g == c)
-            banks[("o", c, a, hh)] = acc
+        def product(c, a, hh, g):
+            if g == 0:
+                banks[("o", c, a, hh)] = psum.tile([P, BANK], F32, name="bank")
+            mx(
+                banks[("o", c, a, hh)][:], ("s", TILES * c + a, g), slice(0, P), ("v", 2 * g + hh), slice(0, BANK),
+                g == 0, g == c,
+            )
 
         def drain(c, a, hh, engine):
             stages[(c, a, hh)] = keep.tile([P, BANK], F32, name="o%d%d%d" % (c, a, hh))
@@ -163,13 +165,13 @@ def tile_simplifiedretnet_pa_kernel(tc, q, k, v, decay, out):
             nc.scalar.dma_start(
                 out=dec[:].rearrange("p (g t) -> p g t", g=2), in_=decay.rearrange("(g p t) -> p g t", g=2, t=TILES)
             )
+        load_values(0, 0)
         load_rows("k", 0)
         load_rows("k", 1)
         load_rows("k", 2)
         load_rows("k", 3)
         load_rows("q", 0)
         load_rows("q", 1)
-        load_values(0, 0)
         load_rows("q", 2)
         load_rows("q", 3)
         load_values(0, 1)
@@ -205,140 +207,147 @@ def tile_simplifiedretnet_pa_kernel(tc, q, k, v, decay, out):
         negd = keep.tile([P, 2 * TILES], F32, name="negd")
         nc.vector.tensor_scalar_mul(out=negd[:], in0=dec[:], scalar1=-1.0)
 
-        turn("k", 0)
-        fetch("k", 0, "vector")
+        regroup(0, "vector")
         table(0, 0, 0)
         table(0, 0, 1)
-        keep_busy(1, 256)
-        turn("k", 1)
-        fetch("k", 1, "scalar")
         table(0, 0, 2)
-        keep_busy(1, 256)
-        turn("k", 2)
-        fetch("k", 2, "vector")
-        quantise("k", 0)
-        keep_busy(1, 256)
-        turn("k", 3)
-        fetch("k", 3, "scalar")
+        turn("k", 0)
+        fetch("k", 0, "scalar")
+        quantise("v", 0)
         table(0, 0, 3)
+        turn("k", 1)
+        fetch("k", 1, "vector")
+        turn("k", 2)
+        fetch("k", 2, "scalar")
+        quantise("k", 0)
+        table(1, 0, 0)
+        turn("k", 3)
+        fetch("k", 3, "vector")
         quantise("k", 1)
-        keep_busy(1, 256)
         turn("q", 0)
-        fetch("q", 0, "vector")
+        fetch("q", 0, "scalar")
         quantise("k", 2)
-        keep_busy(1, 256)
+        table(1, 0, 1)
         turn("q", 1)
-        fetch("q", 1, "scalar")
+        fetch("q", 1, "vector")
         quantise("k", 3)
         quantise("q", 0)
-        table(1, 0, 0)
-        table(1, 0, 1)
-        table(1, 0, 2)
-        scores(0, 0, 0)
         turn("q", 2)
-        quantise("q", 1)
         fetch("q", 2, "scalar")
-        table(1, 0, 3)
-        regroup(0)
-        weigh(0, 0, 0)
-        scores(0, 0, 1)
+        quantise("q", 1)
+        table(1, 0, 2)
         turn("q", 3)
         fetch("q", 3, "scalar")
-        quantise("v", 0)
         quantise("q", 2)
+        table(1, 0, 3)
         table(1, 1, 0)
-        table(1, 1, 1)
+        scores(0, 0, 0)
+        weigh(0, 0, 0)
+        quantise("q", 3)
+        scores(0, 0, 1)
         weigh(0, 0, 1)
         scores(0, 0, 2)
-        quantise("s", 0)
-        quantise("q", 3)
+        weigh(0, 0, 2)
+        quantise("s", 0, 0)
+        scores(0, 0, 3)
+        regroup(1, "vector")
+        weigh(0, 0, 3)
+        table(1, 1, 1)
         turn("q", 4)
         turn("q", 5)
-        weigh(0, 0, 2)
-        fetch("q", 4, "scalar")
-        scores(0, 0, 3)
-        quantise("s", 1)
-        fetch("q", 5, "scalar")
-        regroup(1)
-        weigh(0, 0, 3)
-        quantise("q", 4)
-        table(1, 1, 2)
         turn("q", 6)
         turn("q", 7)
-        scores(1, 0, 0)
+        fetch("q", 4, "scalar")
+        fetch("q", 5, "scalar")
         fetch("q", 6, "scalar")
         fetch("q", 7, "scalar")
+        quantise("s", 1, 0)
+        quantise("q", 4)
         quantise("q", 5)
-        quantise("s", 2)
-        quantise("v", 1)
-        weigh(1, 0, 0)
+        product(0, 0, 0, 0)
+        product(0, 1, 0, 0)
+        drain(0, 0, 0, "scalar")
+        drain(0, 1, 0, "scalar")
+        quantise("s", 2, 0)
+        quantise("s", 3, 0)
+        scores(1, 0, 0)
         scores(1, 0, 1)
-        quantise("s", 3)
         quantise("q", 6)
         quantise("q", 7)
+        table(1, 1, 2)
+        quantise("v", 1)
         turn("k", 4)
         turn("k", 5)
         turn("k", 6)
         turn("k", 7)
-        table(1, 1, 3)
+        weigh(1, 0, 0)
+        weigh(1, 0, 1)
         fetch("k", 4, "scalar")
         fetch("k", 5, "scalar")
-        weigh(1, 0, 1)
-        product(0, 0, 0)
-        product(0, 0, 1)
         fetch("k", 6, "scalar")
         fetch("k", 7, "scalar")
+        product(0, 2, 0, 0)
+        product(0, 3, 0, 0)
         quantise("k", 4)
         quantise("k", 5)
-        regroup(2)
+        quantise("s", 4, 0)
         scores(1, 0, 2)
         scores(1, 0, 3)
-        drain(0, 0, 0, "scalar")
-        drain(0, 0, 1, "scalar")
+        drain(0, 2, 0, "scalar")
+        drain(0, 3, 0, "scalar")
+        regroup(2, "vector")
         quantise("k", 6)
         quantise("k", 7)
+        table(1, 1, 3)
         weigh(1, 0, 2)
-        product(0, 1, 0)
-        product(0, 1, 1)
-        drain(0, 1, 0, "scalar")
+        quantise("s", 5, 0)
+        product(0, 0, 1, 0)
+        product(0, 1, 1, 0)
+        drain(0, 0, 1, "scalar")
         drain(0, 1, 1, "scalar")
-        regroup(3, "scalar")
-        scores(1, 1, 0)
-        weigh(1, 0, 3)
         quantise("v", 2)
-        product(0, 2, 0)
+        weigh(1, 0, 3)
+        scores(1, 1, 0)
         scores(1, 1, 1)
-        product(0, 2, 1)
-        weigh(1, 1, 0)
-        drain(0, 2, 0, "scalar")
-        weigh(1, 1, 1)
-        quantise("s", 4)
-        quantise("v", 3)
-        scores(1, 1, 2)
-        product(0, 3, 0)
+        regroup(3, "vector")
+        product(0, 2, 1, 0)
+        product(0, 3, 1, 0)
         drain(0, 2, 1, "scalar")
-        scores(1, 1, 3)
-        product(0, 3, 1)
-        weigh(1, 1, 2)
-        product(1, 0, 0)
-        product(1, 0, 1)
-        quantise("s", 5)
-        drain(0, 3, 0, "scalar")
         drain(0, 3, 1, "scalar")
-        weigh(1, 1, 3)
-        quantise("s", 6)
-        product(1, 1, 0)
-        product(1, 1, 1)
-        quantise("s", 7)
+        weigh(1, 1, 0)
+        quantise("s", 6, 0)
+        quantise("v", 3)
+        quantise("s", 4, 1)
+        scores(1, 1, 2)
+        scores(1, 1, 3)
+        weigh(1, 1, 1)
+        quantise("s", 7, 0)
+        product(1, 0, 0, 0)
+        product(1, 0, 1, 0)
+        product(1, 0, 0, 1)
+        product(1, 0, 1, 1)
         drain(1, 0, 0, "scalar")
-        drain(1, 0, 1, "vector")
-        product(1, 2, 0)
-        product(1, 2, 1)
+        quantise("s", 5, 1)
+        product(1, 1, 0, 0)
+        product(1, 1, 1, 0)
+        product(1, 1, 0, 1)
+        product(1, 1, 1, 1)
+        weigh(1, 1, 2)
+        drain(1, 0, 1, "scalar")
         drain(1, 1, 0, "scalar")
-        drain(1, 1, 1, "vector")
-        product(1, 3, 0)
-        product(1, 3, 1)
+        weigh(1, 1, 3)
+        quantise("s", 6, 1)
+        drain(1, 1, 1, "scalar")
+        product(1, 2, 0, 0)
+        product(1, 2, 1, 0)
+        product(1, 2, 0, 1)
+        product(1, 2, 1, 1)
+        quantise("s", 7, 1)
         drain(1, 2, 0, "scalar")
         drain(1, 2, 1, "vector")
-        drain(1, 3, 0, "scalar")
-        drain(1, 3, 1, "vector")
+        product(1, 3, 0, 0)
+        product(1, 3, 1, 0)
+        product(1, 3, 0, 1)
+        product(1, 3, 1, 1)
+        drain(1, 3, 0, "vector")
+        drain(1, 3, 1, "scalar")

@@ -162,7 +162,7 @@ def tile_simplifiedretnet_pa_kernel(tc, q, k, v, decay, out):
         keep_busy(6, BANK)
         dec = keep.tile([P, 2 * TILES], BF16, name="dec")
         with nc.allow_non_contiguous_dma(reason="1024 decay rates, four keys to a partition and chunk"):
-            nc.scalar.dma_start(
+            nc.sync.dma_start(
                 out=dec[:].rearrange("p (g t) -> p g t", g=2), in_=decay.rearrange("(g p t) -> p g t", g=2, t=TILES)
             )
         load_values(0, 0)
@@ -190,20 +190,22 @@ def tile_simplifiedretnet_pa_kernel(tc, q, k, v, decay, out):
         nc.vector.memset(warm[:], 0.0)
         warm2 = keep.tile([P, 1], F32, name="warm2")
         nc.scalar.activation(out=warm2[:], in_=warm[:], func=ACT.Exp)
-        ident = keep.tile([P, P], F32, name="ident")
-        make_identity(nc, ident[:])
         dist = keep.tile([P, S + TILES - 1], F32, name="dist")
         near = CHUNK + TILES - 1
-        for y0, y1 in ((0, near), (near, S + TILES - 1)):
-            nc.gpsimd.iota(
-                dist[:, y0:y1], pattern=[[1, y1 - y0]], base=y0 + 1 - TILES, channel_multiplier=-TILES,
-                allow_small_or_imprecise_dtypes=True,
-            )
-            if y0 == 0:
-                nc.gpsimd.affine_select(
-                    out=dist[:, y0:y1], in_=dist[:, y0:y1], pattern=[[1, y1 - y0]], compare_op=ALU.is_ge, fill=FAR,
-                    base=1 - TILES, channel_multiplier=-TILES,
-                )
+        nc.gpsimd.iota(
+            dist[:, 0:near], pattern=[[1, near]], base=1 - TILES, channel_multiplier=-TILES,
+            allow_small_or_imprecise_dtypes=True,
+        )
+        nc.gpsimd.affine_select(
+            out=dist[:, 0:near], in_=dist[:, 0:near], pattern=[[1, near]], compare_op=ALU.is_ge, fill=FAR,
+            base=1 - TILES, channel_multiplier=-TILES,
+        )
+        ident = keep.tile([P, P], F32, name="ident")
+        make_identity(nc, ident[:])
+        nc.gpsimd.iota(
+            dist[:, near : CHUNK + near], pattern=[[1, CHUNK]], base=CHUNK, channel_multiplier=-TILES,
+            allow_small_or_imprecise_dtypes=True,
+        )
         negd = keep.tile([P, 2 * TILES], F32, name="negd")
         nc.vector.tensor_scalar_mul(out=negd[:], in0=dec[:], scalar1=-1.0)
 
@@ -211,23 +213,24 @@ def tile_simplifiedretnet_pa_kernel(tc, q, k, v, decay, out):
         table(0, 0, 0)
         table(0, 0, 1)
         table(0, 0, 2)
+        table(0, 0, 3)
         turn("k", 0)
         fetch("k", 0, "scalar")
         quantise("v", 0)
-        table(0, 0, 3)
+        table(1, 0, 0)
         turn("k", 1)
         fetch("k", 1, "vector")
         turn("k", 2)
         fetch("k", 2, "scalar")
         quantise("k", 0)
-        table(1, 0, 0)
+        table(1, 0, 1)
         turn("k", 3)
         fetch("k", 3, "vector")
         quantise("k", 1)
         turn("q", 0)
         fetch("q", 0, "scalar")
         quantise("k", 2)
-        table(1, 0, 1)
+        table(1, 0, 2)
         turn("q", 1)
         fetch("q", 1, "vector")
         quantise("k", 3)
@@ -235,12 +238,12 @@ def tile_simplifiedretnet_pa_kernel(tc, q, k, v, decay, out):
         turn("q", 2)
         fetch("q", 2, "scalar")
         quantise("q", 1)
-        table(1, 0, 2)
+        table(1, 0, 3)
         turn("q", 3)
         fetch("q", 3, "scalar")
         quantise("q", 2)
-        table(1, 0, 3)
         table(1, 1, 0)
+        table(1, 1, 1)
         scores(0, 0, 0)
         weigh(0, 0, 0)
         quantise("q", 3)
@@ -252,7 +255,7 @@ def tile_simplifiedretnet_pa_kernel(tc, q, k, v, decay, out):
         scores(0, 0, 3)
         regroup(1, "vector")
         weigh(0, 0, 3)
-        table(1, 1, 1)
+        table(1, 1, 2)
         turn("q", 4)
         turn("q", 5)
         turn("q", 6)
@@ -264,90 +267,89 @@ def tile_simplifiedretnet_pa_kernel(tc, q, k, v, decay, out):
         quantise("s", 1, 0)
         quantise("q", 4)
         quantise("q", 5)
-        product(0, 0, 0, 0)
-        product(0, 1, 0, 0)
-        drain(0, 0, 0, "scalar")
-        drain(0, 1, 0, "scalar")
-        quantise("s", 2, 0)
-        quantise("s", 3, 0)
-        scores(1, 0, 0)
-        scores(1, 0, 1)
-        quantise("q", 6)
-        quantise("q", 7)
-        table(1, 1, 2)
-        quantise("v", 1)
         turn("k", 4)
         turn("k", 5)
         turn("k", 6)
         turn("k", 7)
-        weigh(1, 0, 0)
-        weigh(1, 0, 1)
         fetch("k", 4, "scalar")
         fetch("k", 5, "scalar")
         fetch("k", 6, "scalar")
         fetch("k", 7, "scalar")
-        product(0, 2, 0, 0)
-        product(0, 3, 0, 0)
+        quantise("s", 2, 0)
+        quantise("s", 3, 0)
+        quantise("v", 1)
+        quantise("q", 6)
+        quantise("q", 7)
+        product(0, 0, 0, 0)
+        product(0, 1, 0, 0)
+        drain(0, 0, 0, "scalar")
+        drain(0, 1, 0, "scalar")
+        table(1, 1, 3)
+        scores(1, 0, 0)
+        scores(1, 0, 1)
+        regroup(2, "vector")
+        weigh(1, 0, 0)
         quantise("k", 4)
         quantise("k", 5)
-        quantise("s", 4, 0)
-        scores(1, 0, 2)
-        scores(1, 0, 3)
-        drain(0, 2, 0, "scalar")
-        drain(0, 3, 0, "scalar")
-        regroup(2, "vector")
+        weigh(1, 0, 1)
         quantise("k", 6)
         quantise("k", 7)
-        table(1, 1, 3)
-        weigh(1, 0, 2)
-        quantise("s", 5, 0)
         product(0, 0, 1, 0)
         product(0, 1, 1, 0)
         drain(0, 0, 1, "scalar")
         drain(0, 1, 1, "scalar")
-        quantise("v", 2)
-        weigh(1, 0, 3)
+        scores(1, 0, 2)
+        scores(1, 0, 3)
+        quantise("s", 4, 0)
+        weigh(1, 0, 2)
+        quantise("s", 5, 0)
+        regroup(3, "scalar")
         scores(1, 1, 0)
         scores(1, 1, 1)
-        regroup(3, "vector")
-        product(0, 2, 1, 0)
-        product(0, 3, 1, 0)
-        drain(0, 2, 1, "scalar")
-        drain(0, 3, 1, "scalar")
+        weigh(1, 0, 3)
+        quantise("v", 2)
         weigh(1, 1, 0)
         quantise("s", 6, 0)
-        quantise("v", 3)
+        product(0, 2, 0, 0)
+        product(0, 3, 0, 0)
+        product(0, 2, 1, 0)
+        product(0, 3, 1, 0)
+        drain(0, 2, 0, "scalar")
+        drain(0, 3, 0, "scalar")
+        weigh(1, 1, 1)
         quantise("s", 4, 1)
         scores(1, 1, 2)
         scores(1, 1, 3)
-        weigh(1, 1, 1)
-        quantise("s", 7, 0)
         product(1, 0, 0, 0)
         product(1, 0, 1, 0)
         product(1, 0, 0, 1)
-        product(1, 0, 1, 1)
-        drain(1, 0, 0, "scalar")
-        quantise("s", 5, 1)
         product(1, 1, 0, 0)
         product(1, 1, 1, 0)
+        weigh(1, 1, 2)
+        quantise("v", 3)
+        quantise("s", 5, 1)
+        quantise("s", 7, 0)
+        weigh(1, 1, 3)
+        product(1, 0, 1, 1)
+        drain(0, 2, 1, "scalar")
+        drain(0, 3, 1, "scalar")
+        drain(1, 0, 0, "scalar")
         product(1, 1, 0, 1)
         product(1, 1, 1, 1)
-        weigh(1, 1, 2)
-        drain(1, 0, 1, "scalar")
-        drain(1, 1, 0, "scalar")
-        weigh(1, 1, 3)
+        drain(1, 0, 1, "vector")
         quantise("s", 6, 1)
-        drain(1, 1, 1, "scalar")
+        drain(1, 1, 0, "scalar")
+        quantise("s", 7, 1)
+        drain(1, 1, 1, "vector")
         product(1, 2, 0, 0)
         product(1, 2, 1, 0)
         product(1, 2, 0, 1)
         product(1, 2, 1, 1)
-        quantise("s", 7, 1)
         drain(1, 2, 0, "scalar")
         drain(1, 2, 1, "vector")
         product(1, 3, 0, 0)
         product(1, 3, 1, 0)
         product(1, 3, 0, 1)
         product(1, 3, 1, 1)
-        drain(1, 3, 0, "vector")
-        drain(1, 3, 1, "scalar")
+        drain(1, 3, 0, "scalar")
+        drain(1, 3, 1, "vector")

@@ -165,7 +165,6 @@ def tile_simplifiedretnet_pa_kernel(tc, q, k, v, decay, out):
             nc.sync.dma_start(
                 out=dec[:].rearrange("p (g t) -> p g t", g=2), in_=decay.rearrange("(g p t) -> p g t", g=2, t=TILES)
             )
-        load_values(0, 0)
         load_rows("k", 0)
         load_rows("k", 1)
         load_rows("k", 2)
@@ -174,6 +173,7 @@ def tile_simplifiedretnet_pa_kernel(tc, q, k, v, decay, out):
         load_rows("q", 1)
         load_rows("q", 2)
         load_rows("q", 3)
+        load_values(0, 0)
         load_values(0, 1)
         load_rows("q", 4)
         load_rows("q", 5)
@@ -209,147 +209,147 @@ def tile_simplifiedretnet_pa_kernel(tc, q, k, v, decay, out):
         negd = keep.tile([P, 2 * TILES], F32, name="negd")
         nc.vector.tensor_scalar_mul(out=negd[:], in0=dec[:], scalar1=-1.0)
 
-        regroup(0, "vector")
         table(0, 0, 0)
         table(0, 0, 1)
-        table(0, 0, 2)
-        table(0, 0, 3)
         turn("k", 0)
-        fetch("k", 0, "scalar")
-        quantise("v", 0)
-        table(1, 0, 0)
+        fetch("k", 0, "vector")
+        table(0, 0, 2)
         turn("k", 1)
         fetch("k", 1, "vector")
+        table(0, 0, 3)
         turn("k", 2)
         fetch("k", 2, "scalar")
         quantise("k", 0)
-        table(1, 0, 1)
         turn("k", 3)
         fetch("k", 3, "vector")
         quantise("k", 1)
+        table(1, 0, 0)
         turn("q", 0)
         fetch("q", 0, "scalar")
         quantise("k", 2)
-        table(1, 0, 2)
         turn("q", 1)
         fetch("q", 1, "vector")
         quantise("k", 3)
         quantise("q", 0)
+        table(1, 0, 1)
         turn("q", 2)
         fetch("q", 2, "scalar")
         quantise("q", 1)
-        table(1, 0, 3)
         turn("q", 3)
         fetch("q", 3, "scalar")
         quantise("q", 2)
-        table(1, 1, 0)
-        table(1, 1, 1)
+        table(1, 0, 2)
         scores(0, 0, 0)
         weigh(0, 0, 0)
         quantise("q", 3)
         scores(0, 0, 1)
         weigh(0, 0, 1)
         scores(0, 0, 2)
+        table(1, 0, 3)
+        regroup(1, "scalar")
+        regroup(0, "vector")
         weigh(0, 0, 2)
         quantise("s", 0, 0)
         scores(0, 0, 3)
-        regroup(1, "vector")
         weigh(0, 0, 3)
-        table(1, 1, 2)
+        quantise("v", 0)
+        quantise("s", 1, 0)
         turn("q", 4)
         turn("q", 5)
         turn("q", 6)
         turn("q", 7)
-        fetch("q", 4, "scalar")
-        fetch("q", 5, "scalar")
-        fetch("q", 6, "scalar")
-        fetch("q", 7, "scalar")
-        quantise("s", 1, 0)
-        quantise("q", 4)
-        quantise("q", 5)
         turn("k", 4)
         turn("k", 5)
         turn("k", 6)
         turn("k", 7)
+        fetch("q", 4, "scalar")
+        fetch("q", 5, "scalar")
+        quantise("q", 4)
+        quantise("q", 5)
+        quantise("s", 2, 0)
+        product(0, 0, 0, 0)
+        product(0, 1, 0, 0)
+        fetch("q", 6, "scalar")
+        fetch("q", 7, "scalar")
+        quantise("v", 1)
+        quantise("s", 3, 0)
+        table(1, 1, 0)
         fetch("k", 4, "scalar")
         fetch("k", 5, "scalar")
         fetch("k", 6, "scalar")
         fetch("k", 7, "scalar")
-        quantise("s", 2, 0)
-        quantise("s", 3, 0)
-        quantise("v", 1)
         quantise("q", 6)
         quantise("q", 7)
-        product(0, 0, 0, 0)
-        product(0, 1, 0, 0)
-        drain(0, 0, 0, "scalar")
-        drain(0, 1, 0, "scalar")
-        table(1, 1, 3)
+        quantise("k", 4)
+        quantise("k", 5)
+        table(1, 1, 1)
+        table(1, 1, 2)
         scores(1, 0, 0)
         scores(1, 0, 1)
         regroup(2, "vector")
-        weigh(1, 0, 0)
-        quantise("k", 4)
-        quantise("k", 5)
-        weigh(1, 0, 1)
+        product(0, 2, 0, 0)
+        product(0, 0, 1, 0)
+        drain(0, 0, 0, "scalar")
+        drain(0, 1, 0, "scalar")
+        table(1, 1, 3)
         quantise("k", 6)
         quantise("k", 7)
-        product(0, 0, 1, 0)
+        weigh(1, 0, 0)
+        weigh(1, 0, 1)
+        product(0, 3, 0, 0)
         product(0, 1, 1, 0)
+        drain(0, 2, 0, "scalar")
         drain(0, 0, 1, "scalar")
-        drain(0, 1, 1, "scalar")
-        scores(1, 0, 2)
-        scores(1, 0, 3)
-        quantise("s", 4, 0)
-        weigh(1, 0, 2)
-        quantise("s", 5, 0)
-        regroup(3, "scalar")
         scores(1, 1, 0)
         scores(1, 1, 1)
-        weigh(1, 0, 3)
-        quantise("v", 2)
+        regroup(3, "vector")
         weigh(1, 1, 0)
-        quantise("s", 6, 0)
-        product(0, 2, 0, 0)
-        product(0, 3, 0, 0)
-        product(0, 2, 1, 0)
-        product(0, 3, 1, 0)
-        drain(0, 2, 0, "scalar")
-        drain(0, 3, 0, "scalar")
+        quantise("v", 2)
+        quantise("s", 4, 0)
+        scores(1, 0, 2)
+        scores(1, 0, 3)
         weigh(1, 1, 1)
         quantise("s", 4, 1)
+        quantise("v", 3)
+        quantise("s", 5, 0)
+        drain(0, 3, 0, "scalar")
+        drain(0, 1, 1, "scalar")
+        product(0, 2, 1, 0)
+        product(0, 3, 1, 0)
+        product(1, 0, 0, 0)
+        product(1, 0, 0, 1)
+        weigh(1, 0, 2)
+        quantise("s", 5, 1)
+        drain(0, 2, 1, "scalar")
         scores(1, 1, 2)
         scores(1, 1, 3)
-        product(1, 0, 0, 0)
-        product(1, 0, 1, 0)
-        product(1, 0, 0, 1)
-        product(1, 1, 0, 0)
-        product(1, 1, 1, 0)
-        weigh(1, 1, 2)
-        quantise("v", 3)
-        quantise("s", 5, 1)
-        quantise("s", 7, 0)
-        weigh(1, 1, 3)
-        product(1, 0, 1, 1)
-        drain(0, 2, 1, "scalar")
-        drain(0, 3, 1, "scalar")
         drain(1, 0, 0, "scalar")
+        drain(0, 3, 1, "scalar")
+        product(1, 0, 1, 0)
+        product(1, 0, 1, 1)
+        product(1, 1, 0, 0)
         product(1, 1, 0, 1)
+        product(1, 1, 1, 0)
         product(1, 1, 1, 1)
-        drain(1, 0, 1, "vector")
+        weigh(1, 1, 2)
+        quantise("s", 6, 0)
+        weigh(1, 0, 3)
         quantise("s", 6, 1)
+        drain(1, 0, 1, "scalar")
         drain(1, 1, 0, "scalar")
-        quantise("s", 7, 1)
-        drain(1, 1, 1, "vector")
         product(1, 2, 0, 0)
-        product(1, 2, 1, 0)
         product(1, 2, 0, 1)
+        drain(1, 1, 1, "scalar")
+        product(1, 2, 1, 0)
         product(1, 2, 1, 1)
+        weigh(1, 1, 3)
+        quantise("s", 7, 0)
         drain(1, 2, 0, "scalar")
+        quantise("s", 7, 1)
         drain(1, 2, 1, "vector")
         product(1, 3, 0, 0)
         product(1, 3, 1, 0)
         product(1, 3, 0, 1)
         product(1, 3, 1, 1)
-        drain(1, 3, 0, "scalar")
-        drain(1, 3, 1, "vector")
+        drain(1, 3, 0, "vector")
+        drain(1, 3, 1, "scalar")

@@ -1,3 +1,4 @@
+import math
 from contextlib import ExitStack
 
 import concourse.mybir as mybir
@@ -19,6 +20,8 @@ CHUNK = 512
 TILES = CHUNK // P
 BANK = 512
 FAR = 1e30
+RUN = 4
+LOG_SCALE = -math.log(32.0)
 FLOPS = 2 * 2 * H * (CHUNK * CHUNK + CHUNK * 2 * CHUNK)
 
 
@@ -67,7 +70,7 @@ def tile_simplifiedretnet_pa_kernel(tc, q, k, v, decay, out):
             y0 = (0 if g == c else CHUNK) + TILES - 1 - t
             nc.scalar.activation(
                 out=tables[(c, g)][:, CHUNK * t : CHUNK * (t + 1)], in_=dist[:, y0 : y0 + CHUNK], func=ACT.Exp,
-                scale=negd[:, TILES * g + t : TILES * g + t + 1],
+                bias=LOG_SCALE, scale=negd[:, TILES * g + t : TILES * g + t + 1],
             )
 
         def turn(kind, n):
@@ -126,13 +129,12 @@ def tile_simplifiedretnet_pa_kernel(tc, q, k, v, decay, out):
             n = TILES * c + a
             grouped[("s", n, g)] = keep.tile([P, CHUNK], BF16, name="g_s%d%d" % (n, g), align_bytes=64)
             part = grouped[("s", n, g)][:]
-            m = tables[(c, g)][:].rearrange("p (t i) -> p i t", t=TILES)
-            nc.vector.scalar_tensor_tensor(
-                out=part.rearrange("p (i t) -> p i t", t=TILES),
-                in0=banks[(c, g, a)][:].rearrange("p (t i) -> p i t", t=TILES),
-                scalar=1.0 / 32.0,
-                in1=m[:, P * a : P * (a + 1), :],
-                op0=ALU.mult, op1=ALU.mult,
+            m = tables[(c, g)][:].rearrange("p (t e f) -> p e t f", t=TILES, f=RUN)
+            nc.vector.tensor_tensor(
+                out=part.rearrange("p (e f t) -> p e t f", f=RUN, t=TILES),
+                in0=banks[(c, g, a)][:].rearrange("p (t e f) -> p e t f", t=TILES, f=RUN),
+                in1=m[:, P // RUN * a : P // RUN * (a + 1)],
+                op=ALU.mult,
             )
 
         def product(c, a, hh, g):

@@ -230,7 +230,7 @@ def tile_simplifiedretnet_pa_kernel(tc, q, k, v, decay, out):
         fetch("q", 0, "scalar")
         quantise("k", 2)
         turn("q", 1)
-        fetch("q", 1, "vector")
+        fetch("q", 1, "scalar")
         quantise("k", 3)
         quantise("q", 0)
         table(1, 0, 1)
@@ -314,21 +314,21 @@ def tile_simplifiedretnet_pa_kernel(tc, q, k, v, decay, out):
         quantise("s", 4, 1)
         quantise("v", 3)
         quantise("s", 5, 0)
-        drain(0, 3, 0, "scalar")
-        drain(0, 1, 1, "scalar")
         product(0, 2, 1, 0)
         product(0, 3, 1, 0)
+        drain(0, 3, 0, "scalar")
+        drain(0, 1, 1, "scalar")
         product(1, 0, 0, 0)
         product(1, 0, 0, 1)
         weigh(1, 0, 2)
         quantise("s", 5, 1)
         drain(0, 2, 1, "scalar")
         scores(1, 1, 2)
+        product(1, 0, 1, 0)
+        product(1, 0, 1, 1)
         scores(1, 1, 3)
         drain(1, 0, 0, "scalar")
         drain(0, 3, 1, "scalar")
-        product(1, 0, 1, 0)
-        product(1, 0, 1, 1)
         product(1, 1, 0, 0)
         product(1, 1, 0, 1)
         product(1, 1, 1, 0)

import math
from contextlib import ExitStack

import concourse.mybir as mybir
from concourse.masks import make_identity

F32 = mybir.dt.float32
BF16 = mybir.dt.bfloat16
I32 = mybir.dt.int32
U32 = mybir.dt.uint32
U8 = mybir.dt.uint8
FP8X4 = mybir.dt.float8_e4m3fn_x4
ALU = mybir.AluOpType
ACT = mybir.ActivationFunctionType

P = 128
S = 1024
H = 1024
CHUNK = 512
TILES = CHUNK // P
BANK = 512
FAR = 1e30
RUN = 4
LOG_SCALE = -math.log(32.0)
FLOPS = 2 * 2 * H * (CHUNK * CHUNK + CHUNK * 2 * CHUNK)


def tile_simplifiedretnet_pa_kernel(tc, q, k, v, decay, out):
    nc = tc.nc
    dram = {
        "q": q.rearrange("b s h -> (b s) h"),
        "k": k.rearrange("b s h -> (b s) h"),
        "v": v.rearrange("b s h -> (b s) h"),
    }
    out2 = out.rearrange("b s h -> (b s) h")

    with ExitStack() as stack:
        keep = stack.enter_context(tc.tile_pool(name="keep", bufs=1))
        psum = stack.enter_context(tc.psum_pool(name="psum", bufs=8))
        stack.enter_context(tc.manual_schedule())

        raw = {}
        banks = {}
        grouped = {}
        codes = {}
        planes = {}
        tables = {}
        stages = {}

        def load_rows(kind, n):
            raw[(kind, n)] = keep.tile([P, H], BF16, name="raw_%s%d" % (kind, n))
            if kind == "q":
                rows = dram["q"][P * n : P * (n + 1), :]
            else:
                c = n // TILES
                rows = dram["k"][CHUNK * c : CHUNK * (c + 1), :].rearrange("(p t) h -> t p h", t=TILES)[n % TILES]
            nc.sync.dma_start(out=raw[(kind, n)][:], in_=rows)

        def load_values(g, hh):
            raw[("v", 2 * g + hh)] = keep.tile([P, TILES * BANK], BF16, name="raw_v%d%d" % (g, hh))
            rows = dram["v"][CHUNK * g : CHUNK * (g + 1), :].rearrange("(p t) h -> p t h", t=TILES)
            nc.sync.dma_start(
                out=raw[("v", 2 * g + hh)][:].rearrange("p (t h) -> p t h", t=TILES),
                in_=rows[:, :, BANK * hh : BANK * (hh + 1)],
            )

        def table(c, g, t):
            if (c, g) not in tables:
                tables[(c, g)] = keep.tile([P, TILES * CHUNK], F32, name="m%d%d" % (c, g))
            y0 = (0 if g == c else CHUNK) + TILES - 1 - t
            nc.scalar.activation(
                out=tables[(c, g)][:, CHUNK * t : CHUNK * (t + 1)], in_=dist[:, y0 : y0 + CHUNK], func=ACT.Exp,
                bias=LOG_SCALE, scale=negd[:, TILES * g + t : TILES * g + t + 1],
            )

        def turn(kind, n):
            words = raw[(kind, n)][:].bitcast(F32)
            bank = psum.tile([P, BANK], F32, name="bank")
            for w in range(4):
                nc.tensor.transpose(
                    bank[:, P * w : P * (w + 1)], words[:, 2 * P * (w // 2) + w % 2 : 2 * P * (w // 2 + 1) : 2], ident[:]
                )
            banks[(kind, n)] = bank

        def fetch(kind, n, engine):
            grouped[(kind, n)] = keep.tile([P, H], BF16, name="g_%s%d" % (kind, n), align_bytes=64)
            dst = grouped[(kind, n)][:].bitcast(F32).rearrange("p (g r u) -> p g r u", g=2, u=2)
            src = banks[(kind, n)][:].rearrange("p (g u r) -> p g r u", g=2, u=2)
            if engine == "vector":
                nc.vector.tensor_copy(out=dst, in_=src)
            else:
                nc.scalar.copy(out=dst, in_=src)

        def quantise(*key):
            width = grouped[key].shape[1]
            name = "%s%d" % key if len(key) == 2 else "%s%d%d" % key
            cd = keep.tile([P, width // 4], U32, name="c_" + name, align_bytes=64)
            pl = keep.tile([P, width // 4], U8, name="p_" + name, align_bytes=64)
            nc.vector.quantize_mx(out=cd[:].bitcast(FP8X4), scales=pl[:], in_=grouped[key][:])
            codes[key] = cd
            planes[key] = pl

        def regroup(n, engine="vector"):
            grouped[("v", n)] = keep.tile([P, TILES * BANK], BF16, name="g_v%d" % n, align_bytes=64)
            dst = grouped[("v", n)][:].rearrange("p (c i t) -> p c t i", i=4, t=4)
            src = raw[("v", n)][:].rearrange("p (t c i) -> p c t i", t=4, i=4)
            if engine == "vector":
                nc.vector.tensor_copy(out=dst, in_=src)
            else:
                nc.scalar.copy(out=dst, in_=src)

        def mx(dst, left, lcols, right, rcols, start, stop):
            nc.tensor.matmul_mx(
                out=dst,
                lhsT=codes[left][:, lcols].bitcast(FP8X4), lhsT_scale=planes[left][:, lcols],
                rhs=codes[right][:, rcols].bitcast(FP8X4), rhs_scale=planes[right][:, rcols],
                start=start, stop=stop,
            )

        def scores(c, g, a):
            bank = psum.tile([P, BANK], F32, name="bank")
            for t in range(TILES):
                for hp in range(2):
                    cols = slice(P * hp, P * (hp + 1))
                    mx(bank[:, P * t : P * (t + 1)], ("k", TILES * g + t), cols, ("q", TILES * c + a), cols, hp == 0, hp == 1)
            banks[(c, g, a)] = bank

        def weigh(c, g, a):
            n = TILES * c + a
            grouped[("s", n, g)] = keep.tile([P, CHUNK], BF16, name="g_s%d%d" % (n, g), align_bytes=64)
            part = grouped[("s", n, g)][:]
            m = tables[(c, g)][:].rearrange("p (t e f) -> p e t f", t=TILES, f=RUN)
            nc.vector.tensor_tensor(
                out=part.rearrange("p (e f t) -> p e t f", f=RUN, t=TILES),
                in0=banks[(c, g, a)][:].rearrange("p (t e f) -> p e t f", t=TILES, f=RUN),
                in1=m[:, P // RUN * a : P // RUN * (a + 1)],
                op=ALU.mult,
            )

        def product(c, a, hh, g):
            if g == 0:
                banks[("o", c, a, hh)] = psum.tile([P, BANK], F32, name="bank")
            mx(
                banks[("o", c, a, hh)][:], ("s", TILES * c + a, g), slice(0, P), ("v", 2 * g + hh), slice(0, BANK),
                g == 0, g == c,
            )

        def drain(c, a, hh, engine):
            stages[(c, a, hh)] = keep.tile([P, BANK], F32, name="o%d%d%d" % (c, a, hh))
            if engine == "vector":
                nc.vector.tensor_copy(out=stages[(c, a, hh)][:], in_=banks[("o", c, a, hh)][:])
            else:
                nc.scalar.copy(out=stages[(c, a, hh)][:], in_=banks[("o", c, a, hh)][:])
            row = CHUNK * c + P * a
            nc.sync.dma_start(out=out2[row : row + P, BANK * hh : BANK * (hh + 1)], in_=stages[(c, a, hh)][:])

        def keep_busy(count, width):
            bank = psum.tile([P, BANK], F32, name="bank")
            for i in range(count):
                nc.tensor.matmul(out=bank[:, 0:width], lhsT=spin[:, 0:P], rhs=spin[:, 0:width], start=True, stop=True)

        spin = keep.tile([P, BANK], BF16, name="spin")
        nc.vector.memset(spin[:].bitcast(I32), 0)
        keep_busy(6, BANK)
        dec = keep.tile([P, 2 * TILES], BF16, name="dec")
        with nc.allow_non_contiguous_dma(reason="1024 decay rates, four keys to a partition and chunk"):
            nc.sync.dma_start(
                out=dec[:].rearrange("p (g t) -> p g t", g=2), in_=decay.rearrange("(g p t) -> p g t", g=2, t=TILES)
            )
        load_rows("k", 0)
        load_rows("k", 1)
        load_rows("k", 2)
        load_rows("k", 3)
        load_rows("q", 0)
        load_rows("q", 1)
        load_rows("q", 2)
        load_rows("q", 3)
        load_values(0, 0)
        load_values(0, 1)
        load_rows("q", 4)
        load_rows("q", 5)
        load_rows("q", 6)
        load_rows("q", 7)
        load_rows("k", 4)
        load_rows("k", 5)
        load_rows("k", 6)
        load_rows("k", 7)
        load_values(1, 0)
        load_values(1, 1)

        warm = keep.tile([P, 1], F32, name="warm")
        nc.vector.memset(warm[:], 0.0)
        warm2 = keep.tile([P, 1], F32, name="warm2")
        nc.scalar.activation(out=warm2[:], in_=warm[:], func=ACT.Exp)
        dist = keep.tile([P, S + TILES - 1], F32, name="dist")
        near = CHUNK + TILES - 1
        nc.gpsimd.iota(
            dist[:, 0:near], pattern=[[1, near]], base=1 - TILES, channel_multiplier=-TILES,
            allow_small_or_imprecise_dtypes=True,
        )
        nc.gpsimd.affine_select(
            out=dist[:, 0:near], in_=dist[:, 0:near], pattern=[[1, near]], compare_op=ALU.is_ge, fill=FAR,
            base=1 - TILES, channel_multiplier=-TILES,
        )
        ident = keep.tile([P, P], F32, name="ident")
        make_identity(nc, ident[:])
        nc.gpsimd.iota(
            dist[:, near : CHUNK + near], pattern=[[1, CHUNK]], base=CHUNK, channel_multiplier=-TILES,
            allow_small_or_imprecise_dtypes=True,
        )
        negd = keep.tile([P, 2 * TILES], F32, name="negd")
        nc.vector.tensor_scalar_mul(out=negd[:], in0=dec[:], scalar1=-1.0)

        table(0, 0, 0)
        table(0, 0, 1)
        turn("k", 0)
        fetch("k", 0, "vector")
        table(0, 0, 2)
        turn("k", 1)
        fetch("k", 1, "vector")
        table(0, 0, 3)
        turn("k", 2)
        fetch("k", 2, "scalar")
        quantise("k", 0)
        turn("k", 3)
        fetch("k", 3, "vector")
        quantise("k", 1)
        table(1, 0, 0)
        turn("q", 0)
        fetch("q", 0, "scalar")
        quantise("k", 2)
        turn("q", 1)
        fetch("q", 1, "scalar")
        quantise("k", 3)
        quantise("q", 0)
        table(1, 0, 1)
        turn("q", 2)
        fetch("q", 2, "scalar")
        quantise("q", 1)
        turn("q", 3)
        fetch("q", 3, "scalar")
        quantise("q", 2)
        table(1, 0, 2)
        scores(0, 0, 0)
        weigh(0, 0, 0)
        quantise("q", 3)
        scores(0, 0, 1)
        weigh(0, 0, 1)
        scores(0, 0, 2)
        table(1, 0, 3)
        regroup(1, "scalar")
        regroup(0, "vector")
        weigh(0, 0, 2)
        quantise("s", 0, 0)
        scores(0, 0, 3)
        weigh(0, 0, 3)
        quantise("v", 0)
        quantise("s", 1, 0)
        turn("q", 4)
        turn("q", 5)
        turn("q", 6)
        turn("q", 7)
        turn("k", 4)
        turn("k", 5)
        turn("k", 6)
        turn("k", 7)
        fetch("q", 4, "scalar")
        fetch("q", 5, "scalar")
        quantise("q", 4)
        quantise("q", 5)
        quantise("s", 2, 0)
        product(0, 0, 0, 0)
        product(0, 1, 0, 0)
        fetch("q", 6, "scalar")
        fetch("q", 7, "scalar")
        quantise("v", 1)
        quantise("s", 3, 0)
        table(1, 1, 0)
        fetch("k", 4, "scalar")
        fetch("k", 5, "scalar")
        fetch("k", 6, "scalar")
        fetch("k", 7, "scalar")
        quantise("q", 6)
        quantise("q", 7)
        quantise("k", 4)
        quantise("k", 5)
        table(1, 1, 1)
        table(1, 1, 2)
        scores(1, 0, 0)
        scores(1, 0, 1)
        regroup(2, "vector")
        product(0, 2, 0, 0)
        product(0, 0, 1, 0)
        drain(0, 0, 0, "scalar")
        drain(0, 1, 0, "scalar")
        table(1, 1, 3)
        quantise("k", 6)
        quantise("k", 7)
        weigh(1, 0, 0)
        weigh(1, 0, 1)
        product(0, 3, 0, 0)
        product(0, 1, 1, 0)
        drain(0, 2, 0, "scalar")
        drain(0, 0, 1, "scalar")
        scores(1, 1, 0)
        scores(1, 1, 1)
        regroup(3, "vector")
        weigh(1, 1, 0)
        quantise("v", 2)
        quantise("s", 4, 0)
        scores(1, 0, 2)
        scores(1, 0, 3)
        weigh(1, 1, 1)
        quantise("s", 4, 1)
        quantise("v", 3)
        quantise("s", 5, 0)
        product(0, 2, 1, 0)
        product(0, 3, 1, 0)
        drain(0, 3, 0, "scalar")
        drain(0, 1, 1, "scalar")
        product(1, 0, 0, 0)
        product(1, 0, 0, 1)
        weigh(1, 0, 2)
        quantise("s", 5, 1)
        drain(0, 2, 1, "scalar")
        scores(1, 1, 2)
        product(1, 0, 1, 0)
        product(1, 0, 1, 1)
        scores(1, 1, 3)
        drain(1, 0, 0, "scalar")
        drain(0, 3, 1, "scalar")
        product(1, 1, 0, 0)
        product(1, 1, 0, 1)
        product(1, 1, 1, 0)
        product(1, 1, 1, 1)
        weigh(1, 1, 2)
        quantise("s", 6, 0)
        weigh(1, 0, 3)
        quantise("s", 6, 1)
        drain(1, 0, 1, "scalar")
        drain(1, 1, 0, "scalar")
        product(1, 2, 0, 0)
        product(1, 2, 0, 1)
        drain(1, 1, 1, "scalar")
        product(1, 2, 1, 0)
        product(1, 2, 1, 1)
        weigh(1, 1, 3)
        quantise("s", 7, 0)
        drain(1, 2, 0, "scalar")
        quantise("s", 7, 1)
        drain(1, 2, 1, "vector")
        product(1, 3, 0, 0)
        product(1, 3, 1, 0)
        product(1, 3, 0, 1)
        product(1, 3, 1, 1)
        drain(1, 3, 0, "vector")
        drain(1, 3, 1, "scalar")
